import numpy as np
import ml_dtypes


def mxq(x, axis, fmt="e4m3"):
    dtype, down = {"e4m3": (ml_dtypes.float8_e4m3fn, 7), "e5m2": (ml_dtypes.float8_e5m2, 14)}[fmt]
    v = np.moveaxis(np.asarray(x, np.float32).astype(ml_dtypes.bfloat16).astype(np.float64), axis, -1)
    blocks = v.reshape(v.shape[:-1] + (-1, 32))
    amax = np.abs(blocks).max(-1, keepdims=True)
    byte = np.maximum(np.where(amax > 0, np.frexp(amax)[1] - 1 + 127, 0) - down, 1)
    scale = np.exp2(byte - 127.0)
    codes = (blocks / scale).astype(np.float32).astype(dtype).astype(np.float64)
    return np.moveaxis((codes * scale).reshape(v.shape), -1, axis)


WIDE = False


def mx_kscale(k):
    if not WIDE:
        return np.ones(k)
    levels = np.array([10, -10, 5, -5, 0])
    a = np.random.permutation(np.resize(levels, k // 512 * 4)).reshape(k // 512, 4)
    idx = np.arange(k)
    return np.exp2(a[idx // 512, idx % 128 // 32])


BF16 = ml_dtypes.bfloat16


def bf(x):
    return np.asarray(x, np.float32).astype(BF16)


def f64(x):
    return np.asarray(x).astype(np.float64)


H, D, L = 4, 512, 1024
HD = H * D


def split_heads(x):
    return x.reshape(L, H, D).transpose(1, 2, 0)


def setup_inputs():
    s, t = mx_kscale(D), mx_kscale(L)
    tr = np.repeat(t, HD // L)
    e = np.exp(1.5 * np.random.standard_normal((H, L, L)))
    return {"attn": bf(e / e.sum(0, keepdims=True) / t),
            "tokens": bf(np.random.standard_normal((D, L)) * s[:, None]),
            "Wv": bf(np.random.standard_normal((HD, D)) * 0.5 / np.sqrt(D) / s * tr[:, None]),
            "bv": bf(np.random.standard_normal(HD) * 0.15 * tr)}


def reference(attn, tokens, Wv, bv):
    v = split_heads((mxq(f64(Wv), 1, "e4m3") @ mxq(f64(tokens), 0, "e4m3")) + f64(bv)[:, None])
    return mxq(v, 2, "e4m3") @ mxq(f64(attn).transpose(0, 2, 1), 1, "e4m3")

@@ -1,0 +1,266 @@
+from contextlib import ExitStack
+
+import concourse.mybir as mybir
+from concourse.masks import make_identity
+
+F32 = mybir.dt.float32
+BF16 = mybir.dt.bfloat16
+U32 = mybir.dt.uint32
+U8 = mybir.dt.uint8
+FP8X4 = mybir.dt.float8_e4m3fn_x4
+ADD = mybir.AluOpType.add
+
+P = 128
+FLOPS = 2 * 2048 * 1024 * 512 + 2 * 4 * 512 * 1024 * 1024
+
+PIN = False
+
+
+def tile_selfattention_pb_t_kernel(tc, attn, tokens, Wv, bv, out):
+    nc = tc.nc
+    with ExitStack() as ctx:
+        const = ctx.enter_context(tc.tile_pool(name="const", bufs=1))
+        raw = ctx.enter_context(tc.tile_pool(name="raw", bufs=1))
+        codes = ctx.enter_context(tc.tile_pool(name="codes", bufs=1))
+        sgrp = ctx.enter_context(tc.tile_pool(name="sgrp", bufs=6))
+        vgrp = ctx.enter_context(tc.tile_pool(name="vgrp", bufs=4))
+        outp = ctx.enter_context(tc.tile_pool(name="outp", bufs=6))
+        ps_t = ctx.enter_context(tc.psum_pool(name="ps_t", bufs=4))
+        ps_v = ctx.enter_context(tc.psum_pool(name="ps_v", bufs=4))
+        if PIN:
+            ctx.enter_context(tc.manual_schedule())
+
+        wv_view = Wv.rearrange("(gu q ea) k -> gu q (ea k)", gu=4, ea=4)
+        tok_view = tokens.rearrange("(u q e) c -> u q (e c)", u=2, e=2)
+        wv_raw = [raw.tile([P, 2048], BF16, name="wv_raw%d" % gu) for gu in range(4)]
+        tok_raw = raw.tile([P, 4096], BF16, name="tok_raw")
+        at_raw = [raw.tile([P, 4096], BF16, name="at_raw%d" % i) for i in range(8)]
+        bias_raw = const.tile([P, 4, 2, 2], BF16, name="bias_raw")
+        bias_f = const.tile([P, 2, 8], F32, name="bias_f")
+        ident = const.tile([P, P], F32, name="ident")
+
+        with nc.allow_non_contiguous_dma(reason="bias: 8-byte runs, 4 KiB in all"):
+            nc.scalar.dma_start(
+                out=bias_raw[:], in_=bv.rearrange("(gu q e a) -> q gu e a", gu=4, e=2, a=2)
+            )
+        make_identity(nc, ident[:])
+        for gu in (0, 1):
+            nc.sync.dma_start(out=wv_raw[gu][:], in_=wv_view[gu])
+        for u in (0, 1):
+            nc.sync.dma_start(out=tok_raw[:, u * 2048 : (u + 1) * 2048], in_=tok_view[u])
+        for gu in (2, 3):
+            nc.sync.dma_start(out=wv_raw[gu][:], in_=wv_view[gu])
+        for i in range(8):
+            h, lh = divmod(i, 2)
+            nc.sync.dma_start(
+                out=at_raw[i][:],
+                in_=attn[h, lh * 512 : (lh + 1) * 512, :].rearrange("(lp lb) m -> lp (lb m)", lb=4),
+            )
+        for a in (0, 1):
+            nc.vector.tensor_copy(
+                out=bias_f[:, a, :].rearrange("q (gu e) -> q gu e", e=2), in_=bias_raw[:, :, :, a]
+            )
+
+        def code_pair(name):
+            c = codes.tile([P, 512], U32, name=name + "_c", align_bytes=64)
+            s = codes.tile([P, 512], U8, name=name + "_s", align_bytes=64)
+            return c, s
+
+        tok_cs = [code_pair("tok%d" % cb) for cb in range(2)]
+        wv_cs = {(a, g): code_pair("wv%d%d" % (a, g)) for a in range(2) for g in range(2)}
+        at_cs = {(i, g): code_pair("at%d%d" % (i, g)) for i in range(8) for g in range(2)}
+        v_cs = {(h, g): code_pair("v%d%d" % (h, g)) for h in range(4) for g in range(2)}
+
+        def quantise(pair, grp):
+            nc.vector.quantize_mx(out=pair[0][:].bitcast(FP8X4), scales=pair[1][:], in_=grp[:])
+
+        live = {}
+
+        def transposes(key, words, offs):
+            bank = ps_t.tile([P, 512], F32, name="bank_t", tag="t")
+            for n, off in enumerate(offs):
+                nc.tensor.transpose(bank[:, n * P : (n + 1) * P], words[:, off : off + P], ident[:])
+            live[key] = bank
+
+        def evac_words(key, grp, half, eng):
+            bank = live[key]
+            dst = grp[:].bitcast(F32)[:, half * 512 : (half + 1) * 512].rearrange(
+                "p (b c k) -> p b c k", b=2, k=2
+            )
+            src = bank[:].rearrange("p (b k c) -> p b c k", b=2, k=2)
+            if eng == "s":
+                nc.scalar.copy(out=dst, in_=src)
+            else:
+                nc.vector.tensor_copy(out=dst, in_=src)
+
+        def wt_t(a, g, u):
+            words = wv_raw[2 * g + u][:].bitcast(F32)
+            transposes(("wt", a, g, u), words, [(2 * e + a) * 256 + uk * P for e in (0, 1) for uk in (0, 1)])
+
+        def wt_e(a, g, u, eng="s"):
+            if u == 0:
+                live[("wg", a, g)] = sgrp.tile([P, 2048], BF16, name="grp_s", tag="s", align_bytes=64)
+            evac_words(("wt", a, g, u), live[("wg", a, g)], u, eng)
+
+        def wq(a, g):
+            quantise(wv_cs[(a, g)], live[("wg", a, g)])
+
+        def tk_r(cb, eng="v"):
+            tg = vgrp.tile([P, 2048], BF16, name="grp_v", tag="v", align_bytes=64)
+            src = tok_raw[:].rearrange("p (t c) -> p t c", t=4)[:, :, cb * 512 : (cb + 1) * 512]
+            src = src.rearrange("p t (c i) -> p c t i", i=4)
+            dst = tg[:].rearrange("p (c i t) -> p c t i", i=4, t=4)
+            if eng == "v":
+                nc.vector.tensor_copy(out=dst, in_=src)
+            else:
+                nc.scalar.copy(out=dst, in_=src)
+            live[("tg", cb)] = tg
+
+        def tk_q(cb):
+            quantise(tok_cs[cb], live[("tg", cb)])
+
+        def m1(h, g, db):
+            a, cb = divmod(h, 2)
+            bank = ps_v.tile([P, 512], F32, name="bank_v", tag="v")
+            wc, ws = wv_cs[(a, g)]
+            tcd, tsc = tok_cs[cb]
+            for t in range(4):
+                nc.tensor.matmul_mx(
+                    out=bank[:, t * P : (t + 1) * P],
+                    lhsT=wc[:, t * P : (t + 1) * P].bitcast(FP8X4),
+                    lhsT_scale=ws[:, t * P : (t + 1) * P],
+                    rhs=tcd[:, db * P : (db + 1) * P].bitcast(FP8X4),
+                    rhs_scale=tsc[:, db * P : (db + 1) * P],
+                    start=True,
+                    stop=True,
+                )
+            live[("vb", h, g, db)] = bank
+
+        def v_e(h, g, db):
+            a = h // 2
+            if db == 0:
+                live[("vg", h, g)] = vgrp.tile([P, 2048], BF16, name="grp_v", tag="v", align_bytes=64)
+            bank = live[("vb", h, g, db)]
+            nc.vector.tensor_tensor(
+                out=live[("vg", h, g)][:, db * 512 : (db + 1) * 512].rearrange("q (d t) -> q d t", t=4),
+                in0=bank[:].rearrange("q (t d) -> q d t", t=4),
+                in1=bias_f[:, a, 4 * g : 4 * g + 4].unsqueeze(1).to_broadcast([P, P, 4]),
+                op=ADD,
+            )
+
+        def v_q(h, g):
+            quantise(v_cs[(h, g)], live[("vg", h, g)])
+
+        def at_t(i, g, j):
+            words = at_raw[i][:].bitcast(F32)
+            transposes(
+                ("at", i, g, j),
+                words,
+                [(2 * j + b) * 512 + g * 256 + u * P for b in (0, 1) for u in (0, 1)],
+            )
+
+        def at_e(i, g, j, eng="s"):
+            if j == 0:
+                live[("ag", i, g)] = sgrp.tile([P, 2048], BF16, name="grp_s", tag="s", align_bytes=64)
+            evac_words(("at", i, g, j), live[("ag", i, g)], j, eng)
+
+        def a_q(i, g):
+            quantise(at_cs[(i, g)], live[("ag", i, g)])
+
+        def m2(h, db, lh, pool_tag="t"):
+            if pool_tag == "t":
+                bank = ps_t.tile([P, 512], F32, name="bank_t", tag="t")
+            else:
+                bank = ps_v.tile([P, 512], F32, name="bank_v", tag="v")
+            for g in (0, 1):
+                vc, vs = v_cs[(h, g)]
+                ac, asc = at_cs[(2 * h + lh, g)]
+                nc.tensor.matmul_mx(
+                    out=bank[:],
+                    lhsT=vc[:, db * P : (db + 1) * P].bitcast(FP8X4),
+                    lhsT_scale=vs[:, db * P : (db + 1) * P],
+                    rhs=ac[:].bitcast(FP8X4),
+                    rhs_scale=asc[:],
+                    start=(g == 0),
+                    stop=(g == 1),
+                )
+            live[("ob", h, db, lh)] = bank
+
+        def o_e(h, db, lh, eng="s"):
+            if lh == 0:
+                live[("os", h, db)] = outp.tile([P, 1024], F32, name="out_sb", tag="o")
+            bank = live[("ob", h, db, lh)]
+            dst = live[("os", h, db)][:, lh * 512 : (lh + 1) * 512].rearrange("d (lp lb) -> d lp lb", lb=4)
+            src = bank[:].rearrange("d (lb lp) -> d lp lb", lb=4)
+            if eng == "s":
+                nc.scalar.copy(out=dst, in_=src)
+            else:
+                nc.vector.tensor_copy(out=dst, in_=src)
+
+        def store(h, db):
+            nc.sync.dma_start(out=out[h, db * P : (db + 1) * P, :], in_=live[("os", h, db)][:])
+
+        vseq = [(h, g, db) for h in range(4) for g in range(2) for db in range(4)]
+        pos = {"m": 0, "e": 0}
+
+        def run_m1(n):
+            for rep in range(n):
+                if pos["m"] < 32:
+                    m1(*vseq[pos["m"]])
+                    pos["m"] += 1
+
+        def run_ve(n):
+            for rep in range(n):
+                if pos["e"] < pos["m"]:
+                    h, g, db = vseq[pos["e"]]
+                    v_e(h, g, db)
+                    pos["e"] += 1
+                    if db == 3:
+                        v_q(h, g)
+
+        for u in (0, 1):
+            for a in (0, 1):
+                wt_t(a, 0, u)
+                wt_e(a, 0, u)
+        wq(0, 0)
+        tk_r(0)
+        tk_q(0)
+        wq(1, 0)
+        tk_r(1, "s")
+        for u in (0, 1):
+            for a in (0, 1):
+                wt_t(a, 1, u)
+                wt_e(a, 1, u)
+        run_m1(4)
+        run_ve(2)
+        tk_q(1)
+        run_ve(2)
+        wq(0, 1)
+        wq(1, 1)
+        nv = [2, 1, 2, 1, 2, 1, 2, 1]
+        for i in range(8):
+            for g in (0, 1):
+                for j in (0, 1):
+                    at_t(i, g, j)
+                    at_e(i, g, j)
+            run_m1(nv[i])
+            if i >= 1:
+                a_q(i - 1, 0)
+                run_ve(1)
+                a_q(i - 1, 1)
+                run_ve(3)
+            else:
+                run_ve(4)
+        a_q(7, 0)
+        a_q(7, 1)
+        oseq = [(h, db, lh) for h in range(4) for db in range(4) for lh in range(2)]
+        for n, (h, db, lh) in enumerate(oseq):
+            while pos["m"] < (h + 1) * 8:
+                run_m1(1)
+                run_ve(1)
+            run_m1(1)
+            run_ve(1)
+            m2(h, db, lh)
+            o_e(h, db, lh, "v" if (pos["e"] >= 32 and n % 2 == 1) else "s")
+            if lh == 1:
+                store(h, db)

@@ -13,7 +13,7 @@ ADD = mybir.AluOpType.add
 P = 128
 FLOPS = 2 * 2048 * 1024 * 512 + 2 * 4 * 512 * 1024 * 1024
 
-PIN = False
+PIN = True
 
 
 def tile_selfattention_pb_t_kernel(tc, attn, tokens, Wv, bv, out):

@@ -14,6 +14,8 @@ P = 128
 FLOPS = 2 * 2048 * 1024 * 512 + 2 * 4 * 512 * 1024 * 1024
 
 PIN = True
+LEAD = 8
+FIRST_LOADS = 4
 
 
 def tile_selfattention_pb_t_kernel(tc, attn, tokens, Wv, bv, out):
@@ -22,11 +24,13 @@ def tile_selfattention_pb_t_kernel(tc, attn, tokens, Wv, bv, out):
         const = ctx.enter_context(tc.tile_pool(name="const", bufs=1))
         raw = ctx.enter_context(tc.tile_pool(name="raw", bufs=1))
         codes = ctx.enter_context(tc.tile_pool(name="codes", bufs=1))
-        sgrp = ctx.enter_context(tc.tile_pool(name="sgrp", bufs=6))
+        sgrp = ctx.enter_context(tc.tile_pool(name="sgrp", bufs=5))
+        wgrp = ctx.enter_context(tc.tile_pool(name="wgrp", bufs=4))
+        tgrp = ctx.enter_context(tc.tile_pool(name="tgrp", bufs=2))
         vgrp = ctx.enter_context(tc.tile_pool(name="vgrp", bufs=4))
-        outp = ctx.enter_context(tc.tile_pool(name="outp", bufs=6))
+        outp = ctx.enter_context(tc.tile_pool(name="outp", bufs=8))
         ps_t = ctx.enter_context(tc.psum_pool(name="ps_t", bufs=4))
-        ps_v = ctx.enter_context(tc.psum_pool(name="ps_v", bufs=4))
+        ps_b = ctx.enter_context(tc.psum_pool(name="ps_b", bufs=4))
         if PIN:
             ctx.enter_context(tc.manual_schedule())
 
@@ -39,6 +43,13 @@ def tile_selfattention_pb_t_kernel(tc, attn, tokens, Wv, bv, out):
         bias_f = const.tile([P, 2, 8], F32, name="bias_f")
         ident = const.tile([P, P], F32, name="ident")
 
+        def load_attn(i):
+            h, lh = divmod(i, 2)
+            nc.sync.dma_start(
+                out=at_raw[i][:],
+                in_=attn[h, lh * 512 : (lh + 1) * 512, :].rearrange("(lp lb) m -> lp (lb m)", lb=4),
+            )
+
         with nc.allow_non_contiguous_dma(reason="bias: 8-byte runs, 4 KiB in all"):
             nc.scalar.dma_start(
                 out=bias_raw[:], in_=bv.rearrange("(gu q e a) -> q gu e a", gu=4, e=2, a=2)
@@ -50,78 +61,85 @@ def tile_selfattention_pb_t_kernel(tc, attn, tokens, Wv, bv, out):
             nc.sync.dma_start(out=tok_raw[:, u * 2048 : (u + 1) * 2048], in_=tok_view[u])
         for gu in (2, 3):
             nc.sync.dma_start(out=wv_raw[gu][:], in_=wv_view[gu])
-        for i in range(8):
-            h, lh = divmod(i, 2)
-            nc.sync.dma_start(
-                out=at_raw[i][:],
-                in_=attn[h, lh * 512 : (lh + 1) * 512, :].rearrange("(lp lb) m -> lp (lb m)", lb=4),
-            )
+        for i in range(FIRST_LOADS):
+            load_attn(i)
         for a in (0, 1):
             nc.vector.tensor_copy(
                 out=bias_f[:, a, :].rearrange("q (gu e) -> q gu e", e=2), in_=bias_raw[:, :, :, a]
             )
 
-        def code_pair(name):
-            c = codes.tile([P, 512], U32, name=name + "_c", align_bytes=64)
-            s = codes.tile([P, 512], U8, name=name + "_s", align_bytes=64)
+        def code_pair(name, width):
+            c = codes.tile([P, width], U32, name=name + "_c", align_bytes=64)
+            s = codes.tile([P, width], U8, name=name + "_s", align_bytes=64)
             return c, s
 
-        tok_cs = [code_pair("tok%d" % cb) for cb in range(2)]
-        wv_cs = {(a, g): code_pair("wv%d%d" % (a, g)) for a in range(2) for g in range(2)}
-        at_cs = {(i, g): code_pair("at%d%d" % (i, g)) for i in range(8) for g in range(2)}
-        v_cs = {(h, g): code_pair("v%d%d" % (h, g)) for h in range(4) for g in range(2)}
+        tok_cs = [code_pair("tok%d" % cb, 512) for cb in range(2)]
+        wv_cs = {(a, g): code_pair("wv%d%d" % (a, g), 512) for a in range(2) for g in range(2)}
+        at_cs = {(i, g): code_pair("at%d%d" % (i, g), 512) for i in range(8) for g in range(2)}
+        v_cs = {
+            (h, g, k): code_pair("v%d%d%d" % (h, g, k), P)
+            for h in range(4)
+            for g in range(2)
+            for k in range(4)
+        }
 
         def quantise(pair, grp):
             nc.vector.quantize_mx(out=pair[0][:].bitcast(FP8X4), scales=pair[1][:], in_=grp[:])
 
         live = {}
 
-        def transposes(key, words, offs):
-            bank = ps_t.tile([P, 512], F32, name="bank_t", tag="t")
-            for n, off in enumerate(offs):
-                nc.tensor.transpose(bank[:, n * P : (n + 1) * P], words[:, off : off + P], ident[:])
-            live[key] = bank
+        def new_bank(ring):
+            if ring == "t":
+                bank = ps_t.tile([P, 512], F32, name="bank_t", tag="t")
+            else:
+                bank = ps_b.tile([P, 512], F32, name="bank_b", tag="b")
+            return bank
 
-        def evac_words(key, grp, half, eng):
-            bank = live[key]
-            dst = grp[:].bitcast(F32)[:, half * 512 : (half + 1) * 512].rearrange(
-                "p (b c k) -> p b c k", b=2, k=2
-            )
-            src = bank[:].rearrange("p (b k c) -> p b c k", b=2, k=2)
+        def copy_out(eng, dst, src):
             if eng == "s":
                 nc.scalar.copy(out=dst, in_=src)
             else:
                 nc.vector.tensor_copy(out=dst, in_=src)
 
-        def wt_t(a, g, u):
+        def transposes(key, words, offs):
+            bank = new_bank("t")
+            for n, off in enumerate(offs):
+                nc.tensor.transpose(bank[:, n * P : (n + 1) * P], words[:, off : off + P], ident[:])
+            live[key] = bank
+
+        def evac_words(key, grp, half, eng):
+            dst = grp[:].bitcast(F32)[:, half * 512 : (half + 1) * 512].rearrange(
+                "p (b c k) -> p b c k", b=2, k=2
+            )
+            copy_out(eng, dst, live[key][:].rearrange("p (b k c) -> p b c k", b=2, k=2))
+
+        def wt(a, g, u, eng="s"):
             words = wv_raw[2 * g + u][:].bitcast(F32)
             transposes(("wt", a, g, u), words, [(2 * e + a) * 256 + uk * P for e in (0, 1) for uk in (0, 1)])
-
-        def wt_e(a, g, u, eng="s"):
             if u == 0:
-                live[("wg", a, g)] = sgrp.tile([P, 2048], BF16, name="grp_s", tag="s", align_bytes=64)
+                live[("wg", a, g)] = wgrp.tile([P, 2048], BF16, name="grp_w", tag="w", align_bytes=64)
             evac_words(("wt", a, g, u), live[("wg", a, g)], u, eng)
 
         def wq(a, g):
             quantise(wv_cs[(a, g)], live[("wg", a, g)])
 
-        def tk_r(cb, eng="v"):
-            tg = vgrp.tile([P, 2048], BF16, name="grp_v", tag="v", align_bytes=64)
+        def tk_r(cb, eng):
+            tg = tgrp.tile([P, 2048], BF16, name="grp_t", tag="t", align_bytes=64)
             src = tok_raw[:].rearrange("p (t c) -> p t c", t=4)[:, :, cb * 512 : (cb + 1) * 512]
-            src = src.rearrange("p t (c i) -> p c t i", i=4)
-            dst = tg[:].rearrange("p (c i t) -> p c t i", i=4, t=4)
-            if eng == "v":
-                nc.vector.tensor_copy(out=dst, in_=src)
-            else:
-                nc.scalar.copy(out=dst, in_=src)
+            copy_out(
+                eng,
+                tg[:].rearrange("p (c i t) -> p c t i", i=4, t=4),
+                src.rearrange("p t (c i) -> p c t i", i=4),
+            )
             live[("tg", cb)] = tg
 
         def tk_q(cb):
             quantise(tok_cs[cb], live[("tg", cb)])
 
-        def m1(h, g, db):
+        def m1(n):
+            h, g, k = n // 8, (n // 4) % 2, n % 4
             a, cb = divmod(h, 2)
-            bank = ps_v.tile([P, 512], F32, name="bank_v", tag="v")
+            bank = new_bank("b")
             wc, ws = wv_cs[(a, g)]
             tcd, tsc = tok_cs[cb]
             for t in range(4):
@@ -129,138 +147,110 @@ def tile_selfattention_pb_t_kernel(tc, attn, tokens, Wv, bv, out):
                     out=bank[:, t * P : (t + 1) * P],
                     lhsT=wc[:, t * P : (t + 1) * P].bitcast(FP8X4),
                     lhsT_scale=ws[:, t * P : (t + 1) * P],
-                    rhs=tcd[:, db * P : (db + 1) * P].bitcast(FP8X4),
-                    rhs_scale=tsc[:, db * P : (db + 1) * P],
+                    rhs=tcd[:, k * P : (k + 1) * P].bitcast(FP8X4),
+                    rhs_scale=tsc[:, k * P : (k + 1) * P],
                     start=True,
                     stop=True,
                 )
-            live[("vb", h, g, db)] = bank
+            live[("vb", n)] = bank
 
-        def v_e(h, g, db):
-            a = h // 2
-            if db == 0:
-                live[("vg", h, g)] = vgrp.tile([P, 2048], BF16, name="grp_v", tag="v", align_bytes=64)
-            bank = live[("vb", h, g, db)]
+        def ve(n):
+            h, g, k = n // 8, (n // 4) % 2, n % 4
+            vg = vgrp.tile([P, 512], BF16, name="grp_v", tag="v", align_bytes=64)
             nc.vector.tensor_tensor(
-                out=live[("vg", h, g)][:, db * 512 : (db + 1) * 512].rearrange("q (d t) -> q d t", t=4),
-                in0=bank[:].rearrange("q (t d) -> q d t", t=4),
-                in1=bias_f[:, a, 4 * g : 4 * g + 4].unsqueeze(1).to_broadcast([P, P, 4]),
+                out=vg[:].rearrange("q (d t) -> q d t", t=4),
+                in0=live[("vb", n)][:].rearrange("q (t d) -> q d t", t=4),
+                in1=bias_f[:, h // 2, 4 * g : 4 * g + 4].unsqueeze(1).to_broadcast([P, P, 4]),
                 op=ADD,
             )
+            quantise(v_cs[(h, g, k)], vg)
 
-        def v_q(h, g):
-            quantise(v_cs[(h, g)], live[("vg", h, g)])
-
-        def at_t(i, g, j):
+        def at(i):
             words = at_raw[i][:].bitcast(F32)
-            transposes(
-                ("at", i, g, j),
-                words,
-                [(2 * j + b) * 512 + g * 256 + u * P for b in (0, 1) for u in (0, 1)],
-            )
-
-        def at_e(i, g, j, eng="s"):
-            if j == 0:
+            for g in (0, 1):
                 live[("ag", i, g)] = sgrp.tile([P, 2048], BF16, name="grp_s", tag="s", align_bytes=64)
-            evac_words(("at", i, g, j), live[("ag", i, g)], j, eng)
+                for j in (0, 1):
+                    transposes(
+                        ("at", i, g, j),
+                        words,
+                        [(2 * j + b) * 512 + g * 256 + u * P for b in (0, 1) for u in (0, 1)],
+                    )
+                    evac_words(("at", i, g, j), live[("ag", i, g)], j, "s")
 
-        def a_q(i, g):
+        def aq(i, g):
             quantise(at_cs[(i, g)], live[("ag", i, g)])
 
-        def m2(h, db, lh, pool_tag="t"):
-            if pool_tag == "t":
-                bank = ps_t.tile([P, 512], F32, name="bank_t", tag="t")
-            else:
-                bank = ps_v.tile([P, 512], F32, name="bank_v", tag="v")
+        def m2(j, ring, eng):
+            h, lh, k = j // 8, (j // 4) % 2, j % 4
+            bank = new_bank(ring)
             for g in (0, 1):
-                vc, vs = v_cs[(h, g)]
+                vc, vs = v_cs[(h, g, k)]
                 ac, asc = at_cs[(2 * h + lh, g)]
                 nc.tensor.matmul_mx(
                     out=bank[:],
-                    lhsT=vc[:, db * P : (db + 1) * P].bitcast(FP8X4),
-                    lhsT_scale=vs[:, db * P : (db + 1) * P],
+                    lhsT=vc[:].bitcast(FP8X4),
+                    lhsT_scale=vs[:],
                     rhs=ac[:].bitcast(FP8X4),
                     rhs_scale=asc[:],
                     start=(g == 0),
                     stop=(g == 1),
                 )
-            live[("ob", h, db, lh)] = bank
-
-        def o_e(h, db, lh, eng="s"):
-            if lh == 0:
-                live[("os", h, db)] = outp.tile([P, 1024], F32, name="out_sb", tag="o")
-            bank = live[("ob", h, db, lh)]
-            dst = live[("os", h, db)][:, lh * 512 : (lh + 1) * 512].rearrange("d (lp lb) -> d lp lb", lb=4)
-            src = bank[:].rearrange("d (lb lp) -> d lp lb", lb=4)
-            if eng == "s":
-                nc.scalar.copy(out=dst, in_=src)
-            else:
-                nc.vector.tensor_copy(out=dst, in_=src)
-
-        def store(h, db):
-            nc.sync.dma_start(out=out[h, db * P : (db + 1) * P, :], in_=live[("os", h, db)][:])
-
-        vseq = [(h, g, db) for h in range(4) for g in range(2) for db in range(4)]
-        pos = {"m": 0, "e": 0}
-
-        def run_m1(n):
-            for rep in range(n):
-                if pos["m"] < 32:
-                    m1(*vseq[pos["m"]])
-                    pos["m"] += 1
-
-        def run_ve(n):
-            for rep in range(n):
-                if pos["e"] < pos["m"]:
-                    h, g, db = vseq[pos["e"]]
-                    v_e(h, g, db)
-                    pos["e"] += 1
-                    if db == 3:
-                        v_q(h, g)
+            osb = outp.tile([P, 512], F32, name="out_sb", tag="o")
+            copy_out(
+                eng,
+                osb[:].rearrange("d (lp lb) -> d lp lb", lb=4),
+                bank[:].rearrange("d (lb lp) -> d lp lb", lb=4),
+            )
+            nc.sync.dma_start(out=out[h, k * P : (k + 1) * P, lh * 512 : (lh + 1) * 512], in_=osb[:])
 
         for u in (0, 1):
             for a in (0, 1):
-                wt_t(a, 0, u)
-                wt_e(a, 0, u)
+                wt(a, 0, u)
         wq(0, 0)
-        tk_r(0)
+        tk_r(0, "v")
         tk_q(0)
-        wq(1, 0)
         tk_r(1, "s")
-        for u in (0, 1):
-            for a in (0, 1):
-                wt_t(a, 1, u)
-                wt_e(a, 1, u)
-        run_m1(4)
-        run_ve(2)
-        tk_q(1)
-        run_ve(2)
+        for a in (0, 1):
+            wt(a, 1, 0)
+        for n in range(4):
+            m1(n)
+        for a in (0, 1):
+            wt(a, 1, 1)
+        ve(0)
+        ve(1)
+        ve(2)
         wq(0, 1)
-        wq(1, 1)
-        nv = [2, 1, 2, 1, 2, 1, 2, 1]
-        for i in range(8):
-            for g in (0, 1):
-                for j in (0, 1):
-                    at_t(i, g, j)
-                    at_e(i, g, j)
-            run_m1(nv[i])
-            if i >= 1:
-                a_q(i - 1, 0)
-                run_ve(1)
-                a_q(i - 1, 1)
-                run_ve(3)
-            else:
-                run_ve(4)
-        a_q(7, 0)
-        a_q(7, 1)
-        oseq = [(h, db, lh) for h in range(4) for db in range(4) for lh in range(2)]
-        for n, (h, db, lh) in enumerate(oseq):
-            while pos["m"] < (h + 1) * 8:
-                run_m1(1)
-                run_ve(1)
-            run_m1(1)
-            run_ve(1)
-            m2(h, db, lh)
-            o_e(h, db, lh, "v" if (pos["e"] >= 32 and n % 2 == 1) else "s")
-            if lh == 1:
-                store(h, db)
+        ve(3)
+        at(0)
+        for n in range(4, LEAD):
+            m1(n)
+            ve(n)
+            if n == 4:
+                aq(0, 0)
+        aq(0, 1)
+        tk_q(1)
+        at(1)
+        for p in range(8):
+            if p + 2 < 8:
+                at(p + 2)
+            if p + 1 < 8:
+                aq(p + 1, 0)
+                aq(p + 1, 1)
+            for k in range(4):
+                j = 4 * p + k
+                n = j + LEAD
+                late = n >= 32
+                m2(
+                    j,
+                    "t" if (late and p + 2 >= 8 and j % 2 == 1) else "b",
+                    "v" if (late and j % 2 == 1) else "s",
+                )
+                if not late:
+                    m1(n)
+                    ve(n)
+                if p == 0 and k == 1:
+                    wq(1, 0)
+                if p == 0 and k == 3:
+                    wq(1, 1)
+            if p + FIRST_LOADS < 8:
+                load_attn(p + FIRST_LOADS)

@@ -29,8 +29,7 @@ def tile_selfattention_pb_t_kernel(tc, attn, tokens, Wv, bv, out):
         tgrp = ctx.enter_context(tc.tile_pool(name="tgrp", bufs=2))
         vgrp = ctx.enter_context(tc.tile_pool(name="vgrp", bufs=4))
         outp = ctx.enter_context(tc.tile_pool(name="outp", bufs=8))
-        ps_t = ctx.enter_context(tc.psum_pool(name="ps_t", bufs=4))
-        ps_b = ctx.enter_context(tc.psum_pool(name="ps_b", bufs=4))
+        psum = ctx.enter_context(tc.psum_pool(name="psum", bufs=8))
         if PIN:
             ctx.enter_context(tc.manual_schedule())
 
@@ -55,18 +54,12 @@ def tile_selfattention_pb_t_kernel(tc, attn, tokens, Wv, bv, out):
                 out=bias_raw[:], in_=bv.rearrange("(gu q e a) -> q gu e a", gu=4, e=2, a=2)
             )
         make_identity(nc, ident[:])
-        for gu in (0, 1):
-            nc.sync.dma_start(out=wv_raw[gu][:], in_=wv_view[gu])
         for u in (0, 1):
             nc.sync.dma_start(out=tok_raw[:, u * 2048 : (u + 1) * 2048], in_=tok_view[u])
-        for gu in (2, 3):
+        for gu in range(4):
             nc.sync.dma_start(out=wv_raw[gu][:], in_=wv_view[gu])
         for i in range(FIRST_LOADS):
             load_attn(i)
-        for a in (0, 1):
-            nc.vector.tensor_copy(
-                out=bias_f[:, a, :].rearrange("q (gu e) -> q gu e", e=2), in_=bias_raw[:, :, :, a]
-            )
 
         def code_pair(name, width):
             c = codes.tile([P, width], U32, name=name + "_c", align_bytes=64)
@@ -86,13 +79,10 @@ def tile_selfattention_pb_t_kernel(tc, attn, tokens, Wv, bv, out):
         def quantise(pair, grp):
             nc.vector.quantize_mx(out=pair[0][:].bitcast(FP8X4), scales=pair[1][:], in_=grp[:])
 
-        live = {}
+        live = {"waiting": None}
 
-        def new_bank(ring):
-            if ring == "t":
-                bank = ps_t.tile([P, 512], F32, name="bank_t", tag="t")
-            else:
-                bank = ps_b.tile([P, 512], F32, name="bank_b", tag="b")
+        def new_bank():
+            bank = psum.tile([P, 512], F32, name="bank", tag="bank")
             return bank
 
         def copy_out(eng, dst, src):
@@ -102,7 +92,7 @@ def tile_selfattention_pb_t_kernel(tc, attn, tokens, Wv, bv, out):
                 nc.vector.tensor_copy(out=dst, in_=src)
 
         def transposes(key, words, offs):
-            bank = new_bank("t")
+            bank = new_bank()
             for n, off in enumerate(offs):
                 nc.tensor.transpose(bank[:, n * P : (n + 1) * P], words[:, off : off + P], ident[:])
             live[key] = bank
@@ -139,7 +129,7 @@ def tile_selfattention_pb_t_kernel(tc, attn, tokens, Wv, bv, out):
         def m1(n):
             h, g, k = n // 8, (n // 4) % 2, n % 4
             a, cb = divmod(h, 2)
-            bank = new_bank("b")
+            bank = new_bank()
             wc, ws = wv_cs[(a, g)]
             tcd, tsc = tok_cs[cb]
             for t in range(4):
@@ -163,7 +153,13 @@ def tile_selfattention_pb_t_kernel(tc, attn, tokens, Wv, bv, out):
                 in1=bias_f[:, h // 2, 4 * g : 4 * g + 4].unsqueeze(1).to_broadcast([P, P, 4]),
                 op=ADD,
             )
-            quantise(v_cs[(h, g, k)], vg)
+            vq_flush()
+            live["waiting"] = (v_cs[(h, g, k)], vg)
+
+        def vq_flush():
+            if live["waiting"] is not None:
+                quantise(live["waiting"][0], live["waiting"][1])
+            live["waiting"] = None
 
         def at(i):
             words = at_raw[i][:].bitcast(F32)
@@ -180,9 +176,9 @@ def tile_selfattention_pb_t_kernel(tc, attn, tokens, Wv, bv, out):
         def aq(i, g):
             quantise(at_cs[(i, g)], live[("ag", i, g)])
 
-        def m2(j, ring, eng):
+        def m2(j, eng):
             h, lh, k = j // 8, (j // 4) % 2, j % 4
-            bank = new_bank(ring)
+            bank = new_bank()
             for g in (0, 1):
                 vc, vs = v_cs[(h, g, k)]
                 ac, asc = at_cs[(2 * h + lh, g)]
@@ -203,19 +199,24 @@ def tile_selfattention_pb_t_kernel(tc, attn, tokens, Wv, bv, out):
             )
             nc.sync.dma_start(out=out[h, k * P : (k + 1) * P, lh * 512 : (lh + 1) * 512], in_=osb[:])
 
+        tk_r(0, "v")
+        tk_r(1, "v")
+        tk_q(0)
+        tk_q(1)
         for u in (0, 1):
             for a in (0, 1):
                 wt(a, 0, u)
         wq(0, 0)
-        tk_r(0, "v")
-        tk_q(0)
-        tk_r(1, "s")
         for a in (0, 1):
             wt(a, 1, 0)
         for n in range(4):
             m1(n)
         for a in (0, 1):
             wt(a, 1, 1)
+        for a in (0, 1):
+            nc.vector.tensor_copy(
+                out=bias_f[:, a, :].rearrange("q (gu e) -> q gu e", e=2), in_=bias_raw[:, :, :, a]
+            )
         ve(0)
         ve(1)
         ve(2)
@@ -228,7 +229,6 @@ def tile_selfattention_pb_t_kernel(tc, attn, tokens, Wv, bv, out):
             if n == 4:
                 aq(0, 0)
         aq(0, 1)
-        tk_q(1)
         at(1)
         for p in range(8):
             if p + 2 < 8:
@@ -240,11 +240,9 @@ def tile_selfattention_pb_t_kernel(tc, attn, tokens, Wv, bv, out):
                 j = 4 * p + k
                 n = j + LEAD
                 late = n >= 32
-                m2(
-                    j,
-                    "t" if (late and p + 2 >= 8 and j % 2 == 1) else "b",
-                    "v" if (late and j % 2 == 1) else "s",
-                )
+                if late:
+                    vq_flush()
+                m2(j, "v" if (late and j % 2 == 1) else "s")
                 if not late:
                     m1(n)
                     ve(n)

@@ -33,32 +33,48 @@ def tile_selfattention_pb_t_kernel(tc, attn, tokens, Wv, bv, out):
         if PIN:
             ctx.enter_context(tc.manual_schedule())
 
-        wv_view = Wv.rearrange("(gu q ea) k -> gu q (ea k)", gu=4, ea=4)
-        tok_view = tokens.rearrange("(u q e) c -> u q (e c)", u=2, e=2)
-        wv_raw = [raw.tile([P, 2048], BF16, name="wv_raw%d" % gu) for gu in range(4)]
-        tok_raw = raw.tile([P, 4096], BF16, name="tok_raw")
-        at_raw = [raw.tile([P, 4096], BF16, name="at_raw%d" % i) for i in range(8)]
+        wv_view = Wv.rearrange("(gu q e a) k -> gu a q e k", gu=4, e=2, a=2)
+        tok_view = tokens.rearrange("(u q e) c -> u q e c", u=2, e=2)
+        wv_raw = {
+            (a, gu): raw.tile([P, 2, 512], BF16, name="wv_raw%d%d" % (a, gu)) for a in range(2) for gu in range(4)
+        }
+        tok_raw = [raw.tile([P, 4, 512], BF16, name="tok_raw%d" % cb) for cb in range(2)]
+        at_raw = {(i, j): raw.tile([P, 2048], BF16, name="at_raw%d%d" % (i, j)) for i in range(8) for j in range(2)}
         bias_raw = const.tile([P, 4, 2, 2], BF16, name="bias_raw")
         bias_f = const.tile([P, 2, 8], F32, name="bias_f")
         ident = const.tile([P, P], F32, name="ident")
 
         def load_attn(i):
             h, lh = divmod(i, 2)
-            nc.sync.dma_start(
-                out=at_raw[i][:],
-                in_=attn[h, lh * 512 : (lh + 1) * 512, :].rearrange("(lp lb) m -> lp (lb m)", lb=4),
-            )
+            view = attn[h, lh * 512 : (lh + 1) * 512, :].rearrange("(lp j b) m -> j lp (b m)", j=2, b=2)
+            for j in (0, 1):
+                nc.sync.dma_start(out=at_raw[(i, j)][:], in_=view[j])
+
+        def load_wv(a, g):
+            for u in (0, 1):
+                nc.sync.dma_start(out=wv_raw[(a, 2 * g + u)][:], in_=wv_view[2 * g + u][a])
 
         with nc.allow_non_contiguous_dma(reason="bias: 8-byte runs, 4 KiB in all"):
             nc.scalar.dma_start(
                 out=bias_raw[:], in_=bv.rearrange("(gu q e a) -> q gu e a", gu=4, e=2, a=2)
             )
         make_identity(nc, ident[:])
-        for u in (0, 1):
-            nc.sync.dma_start(out=tok_raw[:, u * 2048 : (u + 1) * 2048], in_=tok_view[u])
-        for gu in range(4):
-            nc.sync.dma_start(out=wv_raw[gu][:], in_=wv_view[gu])
-        for i in range(FIRST_LOADS):
+        def load_tokens(cb):
+            for u in (0, 1):
+                nc.sync.dma_start(
+                    out=tok_raw[cb][:, 2 * u : 2 * u + 2, :],
+                    in_=tok_view[u][:, :, cb * 512 : (cb + 1) * 512],
+                )
+
+        load_wv(0, 0)
+        load_tokens(0)
+        load_wv(0, 1)
+        load_attn(0)
+        load_tokens(1)
+        load_attn(1)
+        load_wv(1, 0)
+        load_wv(1, 1)
+        for i in range(2, FIRST_LOADS):
             load_attn(i)
 
         def code_pair(name, width):
@@ -104,8 +120,8 @@ def tile_selfattention_pb_t_kernel(tc, attn, tokens, Wv, bv, out):
             copy_out(eng, dst, live[key][:].rearrange("p (b k c) -> p b c k", b=2, k=2))
 
         def wt(a, g, u, eng="s"):
-            words = wv_raw[2 * g + u][:].bitcast(F32)
-            transposes(("wt", a, g, u), words, [(2 * e + a) * 256 + uk * P for e in (0, 1) for uk in (0, 1)])
+            words = wv_raw[(a, 2 * g + u)][:].rearrange("q e k -> q (e k)").bitcast(F32)
+            transposes(("wt", a, g, u), words, [e * 256 + uk * P for e in (0, 1) for uk in (0, 1)])
             if u == 0:
                 live[("wg", a, g)] = wgrp.tile([P, 2048], BF16, name="grp_w", tag="w", align_bytes=64)
             evac_words(("wt", a, g, u), live[("wg", a, g)], u, eng)
@@ -115,11 +131,10 @@ def tile_selfattention_pb_t_kernel(tc, attn, tokens, Wv, bv, out):
 
         def tk_r(cb, eng):
             tg = tgrp.tile([P, 2048], BF16, name="grp_t", tag="t", align_bytes=64)
-            src = tok_raw[:].rearrange("p (t c) -> p t c", t=4)[:, :, cb * 512 : (cb + 1) * 512]
             copy_out(
                 eng,
                 tg[:].rearrange("p (c i t) -> p c t i", i=4, t=4),
-                src.rearrange("p t (c i) -> p c t i", i=4),
+                tok_raw[cb][:].rearrange("p t (c i) -> p c t i", i=4),
             )
             live[("tg", cb)] = tg
 
@@ -162,14 +177,15 @@ def tile_selfattention_pb_t_kernel(tc, attn, tokens, Wv, bv, out):
             live["waiting"] = None
 
         def at(i):
-            words = at_raw[i][:].bitcast(F32)
             for g in (0, 1):
                 live[("ag", i, g)] = sgrp.tile([P, 2048], BF16, name="grp_s", tag="s", align_bytes=64)
-                for j in (0, 1):
+            for j in (0, 1):
+                words = at_raw[(i, j)][:].bitcast(F32)
+                for g in (0, 1):
                     transposes(
                         ("at", i, g, j),
                         words,
-                        [(2 * j + b) * 512 + g * 256 + u * P for b in (0, 1) for u in (0, 1)],
+                        [b * 512 + g * 256 + u * P for b in (0, 1) for u in (0, 1)],
                     )
                     evac_words(("at", i, g, j), live[("ag", i, g)], j, "s")
 
@@ -199,37 +215,35 @@ def tile_selfattention_pb_t_kernel(tc, attn, tokens, Wv, bv, out):
             )
             nc.sync.dma_start(out=out[h, k * P : (k + 1) * P, lh * 512 : (lh + 1) * 512], in_=osb[:])
 
+        for g in (0, 1):
+            for u in (0, 1):
+                wt(0, g, u)
         tk_r(0, "v")
-        tk_r(1, "v")
-        tk_q(0)
-        tk_q(1)
-        for u in (0, 1):
-            for a in (0, 1):
-                wt(a, 0, u)
         wq(0, 0)
-        for a in (0, 1):
-            wt(a, 1, 0)
+        tk_q(0)
         for n in range(4):
             m1(n)
-        for a in (0, 1):
-            wt(a, 1, 1)
         for a in (0, 1):
             nc.vector.tensor_copy(
                 out=bias_f[:, a, :].rearrange("q (gu e) -> q gu e", e=2), in_=bias_raw[:, :, :, a]
             )
         ve(0)
         ve(1)
-        ve(2)
         wq(0, 1)
+        ve(2)
         ve(3)
+        tk_r(1, "v")
         at(0)
         for n in range(4, LEAD):
             m1(n)
             ve(n)
-            if n == 4:
-                aq(0, 0)
+        aq(0, 0)
+        tk_q(1)
         aq(0, 1)
         at(1)
+        for g in (0, 1):
+            for u in (0, 1):
+                wt(1, g, u)
         for p in range(8):
             if p + 2 < 8:
                 at(p + 2)
@@ -239,13 +253,12 @@ def tile_selfattention_pb_t_kernel(tc, attn, tokens, Wv, bv, out):
             for k in range(4):
                 j = 4 * p + k
                 n = j + LEAD
-                late = n >= 32
-                if late:
-                    vq_flush()
-                m2(j, "v" if (late and j % 2 == 1) else "s")
-                if not late:
+                m2(j, "v" if (n >= 32 and j % 2 == 1) else "s")
+                if n < 32:
                     m1(n)
                     ve(n)
+                if n == 31:
+                    vq_flush()
                 if p == 0 and k == 1:
                     wq(1, 0)
                 if p == 0 and k == 3:

@@ -176,10 +176,11 @@ def tile_selfattention_pb_t_kernel(tc, attn, tokens, Wv, bv, out):
                 quantise(live["waiting"][0], live["waiting"][1])
             live["waiting"] = None
 
-        def at(i):
-            for g in (0, 1):
-                live[("ag", i, g)] = sgrp.tile([P, 2048], BF16, name="grp_s", tag="s", align_bytes=64)
-            for j in (0, 1):
+        def at(i, halves=(0, 1)):
+            if 0 in halves:
+                for g in (0, 1):
+                    live[("ag", i, g)] = sgrp.tile([P, 2048], BF16, name="grp_s", tag="s", align_bytes=64)
+            for j in halves:
                 words = at_raw[(i, j)][:].bitcast(F32)
                 for g in (0, 1):
                     transposes(
@@ -246,11 +247,13 @@ def tile_selfattention_pb_t_kernel(tc, attn, tokens, Wv, bv, out):
                 wt(1, g, u)
         for p in range(8):
             if p + 2 < 8:
-                at(p + 2)
+                at(p + 2, (0,))
             if p + 1 < 8:
                 aq(p + 1, 0)
                 aq(p + 1, 1)
             for k in range(4):
+                if k == 2 and p + 2 < 8:
+                    at(p + 2, (1,))
                 j = 4 * p + k
                 n = j + LEAD
                 m2(j, "v" if (n >= 32 and j % 2 == 1) else "s")

@@ -250,10 +250,11 @@ def tile_selfattention_pb_t_kernel(tc, attn, tokens, Wv, bv, out):
                 at(p + 2, (0,))
             if p + 1 < 8:
                 aq(p + 1, 0)
-                aq(p + 1, 1)
             for k in range(4):
                 if k == 2 and p + 2 < 8:
                     at(p + 2, (1,))
+                if k == 2 and p + 1 < 8:
+                    aq(p + 1, 1)
                 j = 4 * p + k
                 n = j + LEAD
                 m2(j, "v" if (n >= 32 and j % 2 == 1) else "s")

@@ -246,15 +246,21 @@ def tile_selfattention_pb_t_kernel(tc, attn, tokens, Wv, bv, out):
             for u in (0, 1):
                 wt(1, g, u)
         for p in range(8):
-            if p + 2 < 8:
+            if p < 4:
                 at(p + 2, (0,))
-            if p + 1 < 8:
+            if p in (5, 6):
+                at(p + 1)
+            if p < 5:
                 aq(p + 1, 0)
             for k in range(4):
-                if k == 2 and p + 2 < 8:
+                if k == 2 and p < 4:
                     at(p + 2, (1,))
-                if k == 2 and p + 1 < 8:
+                if k == 2 and p < 5:
                     aq(p + 1, 1)
+                if p == 5 and k >= 2:
+                    aq(6, k - 2)
+                if p == 6 and k in (1, 2):
+                    aq(7, k - 1)
                 j = 4 * p + k
                 n = j + LEAD
                 m2(j, "v" if (n >= 32 and j % 2 == 1) else "s")

from contextlib import ExitStack

import concourse.mybir as mybir
from concourse.masks import make_identity

F32 = mybir.dt.float32
BF16 = mybir.dt.bfloat16
U32 = mybir.dt.uint32
U8 = mybir.dt.uint8
FP8X4 = mybir.dt.float8_e4m3fn_x4
ADD = mybir.AluOpType.add

P = 128
FLOPS = 2 * 2048 * 1024 * 512 + 2 * 4 * 512 * 1024 * 1024

PIN = True
LEAD = 8
FIRST_LOADS = 4


def tile_selfattention_pb_t_kernel(tc, attn, tokens, Wv, bv, out):
    nc = tc.nc
    with ExitStack() as ctx:
        const = ctx.enter_context(tc.tile_pool(name="const", bufs=1))
        raw = ctx.enter_context(tc.tile_pool(name="raw", bufs=1))
        codes = ctx.enter_context(tc.tile_pool(name="codes", bufs=1))
        sgrp = ctx.enter_context(tc.tile_pool(name="sgrp", bufs=5))
        wgrp = ctx.enter_context(tc.tile_pool(name="wgrp", bufs=4))
        tgrp = ctx.enter_context(tc.tile_pool(name="tgrp", bufs=2))
        vgrp = ctx.enter_context(tc.tile_pool(name="vgrp", bufs=4))
        outp = ctx.enter_context(tc.tile_pool(name="outp", bufs=8))
        psum = ctx.enter_context(tc.psum_pool(name="psum", bufs=8))
        if PIN:
            ctx.enter_context(tc.manual_schedule())

        wv_view = Wv.rearrange("(gu q e a) k -> gu a q e k", gu=4, e=2, a=2)
        tok_view = tokens.rearrange("(u q e) c -> u q e c", u=2, e=2)
        wv_raw = {
            (a, gu): raw.tile([P, 2, 512], BF16, name="wv_raw%d%d" % (a, gu)) for a in range(2) for gu in range(4)
        }
        tok_raw = [raw.tile([P, 4, 512], BF16, name="tok_raw%d" % cb) for cb in range(2)]
        at_raw = {(i, j): raw.tile([P, 2048], BF16, name="at_raw%d%d" % (i, j)) for i in range(8) for j in range(2)}
        bias_raw = const.tile([P, 4, 2, 2], BF16, name="bias_raw")
        bias_f = const.tile([P, 2, 8], F32, name="bias_f")
        ident = const.tile([P, P], F32, name="ident")

        def load_attn(i):
            h, lh = divmod(i, 2)
            view = attn[h, lh * 512 : (lh + 1) * 512, :].rearrange("(lp j b) m -> j lp (b m)", j=2, b=2)
            for j in (0, 1):
                nc.sync.dma_start(out=at_raw[(i, j)][:], in_=view[j])

        def load_wv(a, g):
            for u in (0, 1):
                nc.sync.dma_start(out=wv_raw[(a, 2 * g + u)][:], in_=wv_view[2 * g + u][a])

        with nc.allow_non_contiguous_dma(reason="bias: 8-byte runs, 4 KiB in all"):
            nc.scalar.dma_start(
                out=bias_raw[:], in_=bv.rearrange("(gu q e a) -> q gu e a", gu=4, e=2, a=2)
            )
        make_identity(nc, ident[:])
        def load_tokens(cb):
            for u in (0, 1):
                nc.sync.dma_start(
                    out=tok_raw[cb][:, 2 * u : 2 * u + 2, :],
                    in_=tok_view[u][:, :, cb * 512 : (cb + 1) * 512],
                )

        load_wv(0, 0)
        load_tokens(0)
        load_wv(0, 1)
        load_attn(0)
        load_tokens(1)
        load_attn(1)
        load_wv(1, 0)
        load_wv(1, 1)
        for i in range(2, FIRST_LOADS):
            load_attn(i)

        def code_pair(name, width):
            c = codes.tile([P, width], U32, name=name + "_c", align_bytes=64)
            s = codes.tile([P, width], U8, name=name + "_s", align_bytes=64)
            return c, s

        tok_cs = [code_pair("tok%d" % cb, 512) for cb in range(2)]
        wv_cs = {(a, g): code_pair("wv%d%d" % (a, g), 512) for a in range(2) for g in range(2)}
        at_cs = {(i, g): code_pair("at%d%d" % (i, g), 512) for i in range(8) for g in range(2)}
        v_cs = {
            (h, g, k): code_pair("v%d%d%d" % (h, g, k), P)
            for h in range(4)
            for g in range(2)
            for k in range(4)
        }

        def quantise(pair, grp):
            nc.vector.quantize_mx(out=pair[0][:].bitcast(FP8X4), scales=pair[1][:], in_=grp[:])

        live = {"waiting": None}

        def new_bank():
            bank = psum.tile([P, 512], F32, name="bank", tag="bank")
            return bank

        def copy_out(eng, dst, src):
            if eng == "s":
                nc.scalar.copy(out=dst, in_=src)
            else:
                nc.vector.tensor_copy(out=dst, in_=src)

        def transposes(key, words, offs):
            bank = new_bank()
            for n, off in enumerate(offs):
                nc.tensor.transpose(bank[:, n * P : (n + 1) * P], words[:, off : off + P], ident[:])
            live[key] = bank

        def evac_words(key, grp, half, eng):
            dst = grp[:].bitcast(F32)[:, half * 512 : (half + 1) * 512].rearrange(
                "p (b c k) -> p b c k", b=2, k=2
            )
            copy_out(eng, dst, live[key][:].rearrange("p (b k c) -> p b c k", b=2, k=2))

        def wt(a, g, u, eng="s"):
            words = wv_raw[(a, 2 * g + u)][:].rearrange("q e k -> q (e k)").bitcast(F32)
            transposes(("wt", a, g, u), words, [e * 256 + uk * P for e in (0, 1) for uk in (0, 1)])
            if u == 0:
                live[("wg", a, g)] = wgrp.tile([P, 2048], BF16, name="grp_w", tag="w", align_bytes=64)
            evac_words(("wt", a, g, u), live[("wg", a, g)], u, eng)

        def wq(a, g):
            quantise(wv_cs[(a, g)], live[("wg", a, g)])

        def tk_r(cb, eng):
            tg = tgrp.tile([P, 2048], BF16, name="grp_t", tag="t", align_bytes=64)
            copy_out(
                eng,
                tg[:].rearrange("p (c i t) -> p c t i", i=4, t=4),
                tok_raw[cb][:].rearrange("p t (c i) -> p c t i", i=4),
            )
            live[("tg", cb)] = tg

        def tk_q(cb):
            quantise(tok_cs[cb], live[("tg", cb)])

        def m1(n):
            h, g, k = n // 8, (n // 4) % 2, n % 4
            a, cb = divmod(h, 2)
            bank = new_bank()
            wc, ws = wv_cs[(a, g)]
            tcd, tsc = tok_cs[cb]
            for t in range(4):
                nc.tensor.matmul_mx(
                    out=bank[:, t * P : (t + 1) * P],
                    lhsT=wc[:, t * P : (t + 1) * P].bitcast(FP8X4),
                    lhsT_scale=ws[:, t * P : (t + 1) * P],
                    rhs=tcd[:, k * P : (k + 1) * P].bitcast(FP8X4),
                    rhs_scale=tsc[:, k * P : (k + 1) * P],
                    start=True,
                    stop=True,
                )
            live[("vb", n)] = bank

        def ve(n):
            h, g, k = n // 8, (n // 4) % 2, n % 4
            vg = vgrp.tile([P, 512], BF16, name="grp_v", tag="v", align_bytes=64)
            nc.vector.tensor_tensor(
                out=vg[:].rearrange("q (d t) -> q d t", t=4),
                in0=live[("vb", n)][:].rearrange("q (t d) -> q d t", t=4),
                in1=bias_f[:, h // 2, 4 * g : 4 * g + 4].unsqueeze(1).to_broadcast([P, P, 4]),
                op=ADD,
            )
            vq_flush()
            live["waiting"] = (v_cs[(h, g, k)], vg)

        def vq_flush():
            if live["waiting"] is not None:
                quantise(live["waiting"][0], live["waiting"][1])
            live["waiting"] = None

        def at(i, halves=(0, 1)):
            if 0 in halves:
                for g in (0, 1):
                    live[("ag", i, g)] = sgrp.tile([P, 2048], BF16, name="grp_s", tag="s", align_bytes=64)
            for j in halves:
                words = at_raw[(i, j)][:].bitcast(F32)
                for g in (0, 1):
                    transposes(
                        ("at", i, g, j),
                        words,
                        [b * 512 + g * 256 + u * P for b in (0, 1) for u in (0, 1)],
                    )
                    evac_words(("at", i, g, j), live[("ag", i, g)], j, "s")

        def aq(i, g):
            quantise(at_cs[(i, g)], live[("ag", i, g)])

        def m2(j, eng):
            h, lh, k = j // 8, (j // 4) % 2, j % 4
            bank = new_bank()
            for g in (0, 1):
                vc, vs = v_cs[(h, g, k)]
                ac, asc = at_cs[(2 * h + lh, g)]
                nc.tensor.matmul_mx(
                    out=bank[:],
                    lhsT=vc[:].bitcast(FP8X4),
                    lhsT_scale=vs[:],
                    rhs=ac[:].bitcast(FP8X4),
                    rhs_scale=asc[:],
                    start=(g == 0),
                    stop=(g == 1),
                )
            osb = outp.tile([P, 512], F32, name="out_sb", tag="o")
            copy_out(
                eng,
                osb[:].rearrange("d (lp lb) -> d lp lb", lb=4),
                bank[:].rearrange("d (lb lp) -> d lp lb", lb=4),
            )
            nc.sync.dma_start(out=out[h, k * P : (k + 1) * P, lh * 512 : (lh + 1) * 512], in_=osb[:])

        for g in (0, 1):
            for u in (0, 1):
                wt(0, g, u)
        tk_r(0, "v")
        wq(0, 0)
        tk_q(0)
        for n in range(4):
            m1(n)
        for a in (0, 1):
            nc.vector.tensor_copy(
                out=bias_f[:, a, :].rearrange("q (gu e) -> q gu e", e=2), in_=bias_raw[:, :, :, a]
            )
        ve(0)
        ve(1)
        wq(0, 1)
        ve(2)
        ve(3)
        tk_r(1, "v")
        at(0)
        for n in range(4, LEAD):
            m1(n)
            ve(n)
        aq(0, 0)
        tk_q(1)
        aq(0, 1)
        at(1)
        for g in (0, 1):
            for u in (0, 1):
                wt(1, g, u)
        for p in range(8):
            if p < 4:
                at(p + 2, (0,))
            if p in (5, 6):
                at(p + 1)
            if p < 5:
                aq(p + 1, 0)
            for k in range(4):
                if k == 2 and p < 4:
                    at(p + 2, (1,))
                if k == 2 and p < 5:
                    aq(p + 1, 1)
                if p == 5 and k >= 2:
                    aq(6, k - 2)
                if p == 6 and k in (1, 2):
                    aq(7, k - 1)
                j = 4 * p + k
                n = j + LEAD
                m2(j, "v" if (n >= 32 and j % 2 == 1) else "s")
                if n < 32:
                    m1(n)
                    ve(n)
                if n == 31:
                    vq_flush()
                if p == 0 and k == 1:
                    wq(1, 0)
                if p == 0 and k == 3:
                    wq(1, 1)
            if p + FIRST_LOADS < 8:
                load_attn(p + FIRST_LOADS)
